import numpy as np
import ml_dtypes

BF16 = ml_dtypes.bfloat16


def bf(x):
    return np.asarray(x, np.float32).astype(BF16)


def f32(x):
    return np.asarray(x, np.float32)


def f64(x):
    return np.asarray(x).astype(np.float64)


def striped(idx):
    return np.tile(idx.reshape(-1, 16).T, (8, 1))


C, K, S, N = 256, 512, 4096, 2048


def sigmoid(v):
    return 1.0 / (1.0 + np.exp(-v))


def setup_inputs():
    return {"base": f32(np.random.standard_normal((C, S))), "h": f32(np.random.standard_normal((C, N))), "inp": f32(np.random.standard_normal((C, N))), "wzr": bf(np.random.standard_normal((K, K)) / np.sqrt(K)), "wt": bf(np.random.standard_normal((K, C)) / np.sqrt(K)), "offs": striped(np.random.permutation(S)[:N])}


def reference(base, h, inp, wzr, wt, offs):
    idx = offs[:16].T.reshape(-1)
    hh = f64(h)
    ii = f64(inp)
    pre = f64(wzr).T @ np.concatenate([hh, ii], axis=0)
    z = sigmoid(pre[:C])
    r = sigmoid(pre[C:])
    t = np.tanh(f64(wt).T @ np.concatenate([r * hh, ii], axis=0))
    out = f64(base).copy()
    out[:, idx] = (1.0 - z) * hh + z * t
    return out

@@ -1,0 +1,113 @@
+import concourse.mybir as mybir
+
+P = 128
+C, K, S, N = 256, 512, 4096, 2048
+CB = C // P
+KB = K // P
+PIECE = 512
+NP = N // PIECE
+K_ORDER = (2, 3, 0, 1)
+
+FLOPS = 2 * K * (K + C) * N
+
+F32, BF16, U16 = mybir.dt.float32, mybir.dt.bfloat16, mybir.dt.uint16
+
+
+def tile_graphnn_kernel(tc, base, h, inp, wzr, wt, offs, out):
+    nc = tc.nc
+    sigmoid = mybir.ActivationFunctionType.Sigmoid
+    tanh = mybir.ActivationFunctionType.Tanh
+    mult, add = mybir.AluOpType.mult, mybir.AluOpType.add
+
+    with (
+        tc.tile_pool(name="held", bufs=1) as held,
+        tc.tile_pool(name="gates", bufs=4) as gates,
+        tc.psum_pool(name="psum", bufs=8) as psum,
+    ):
+        offsets = held.tile([P, N // 16], U16, name="offsets")
+        nc.sync.dma_start(offsets[:], offs)
+
+        wzr_sb = held.tile([P, KB, K], BF16, name="wzr_sb")
+        nc.sync.dma_start(wzr_sb[:], wzr.rearrange("(kb p) m -> p kb m", p=P))
+        wt_sb = held.tile([P, KB, C], BF16, name="wt_sb")
+        nc.scalar.dma_start(wt_sb[:], wt.rearrange("(kb p) m -> p kb m", p=P))
+
+        h_f32 = [held.tile([P, N], F32, name=f"h_f32_{b}") for b in range(CB)]
+        inp_f32 = [held.tile([P, N], F32, name=f"inp_f32_{b}") for b in range(CB)]
+        for n in range(NP):
+            cols = slice(n * PIECE, (n + 1) * PIECE)
+            for b in range(CB):
+                rows = slice(b * P, (b + 1) * P)
+                nc.sync.dma_start(h_f32[b][:, cols], h[rows, cols])
+                nc.scalar.dma_start(inp_f32[b][:, cols], inp[rows, cols])
+
+        window = [held.tile([P, S], F32, name=f"window_{b}") for b in range(CB)]
+        for b in range(CB):
+            nc.sync.dma_start(window[b][:], base[b * P : (b + 1) * P, :])
+
+        h_bf = [held.tile([P, N], BF16, name=f"h_bf_{b}") for b in range(CB)]
+        inp_bf = [held.tile([P, N], BF16, name=f"inp_bf_{b}") for b in range(CB)]
+        rh_bf = [held.tile([P, N], BF16, name=f"rh_bf_{b}") for b in range(CB)]
+        z_f32 = [held.tile([P, N], F32, name=f"z_f32_{b}") for b in range(CB)]
+        kept = [held.tile([P, N], F32, name=f"kept_{b}") for b in range(CB)]
+        fresh = [held.tile([P, N], F32, name=f"fresh_{b}") for b in range(CB)]
+        x = h_bf + inp_bf
+        y = rh_bf + inp_bf
+
+        product_engine = (nc.vector, nc.gpsimd)
+
+        def matmul_piece(weights, first_col, moving, cols):
+            bank = psum.tile([P, PIECE], F32, name="bank")
+            for step, kb in enumerate(K_ORDER):
+                nc.tensor.matmul(
+                    bank[:],
+                    weights[:, kb, first_col : first_col + P],
+                    moving[kb][:, cols],
+                    start=(step == 0),
+                    stop=(step == KB - 1),
+                )
+            return bank
+
+        def reset_gate(b, cols):
+            bank = matmul_piece(wzr_sb, C + b * P, x, cols)
+            r = gates.tile([P, PIECE], F32, name="r")
+            nc.scalar.activation(r[:], bank[:], sigmoid)
+            nc.vector.tensor_tensor(rh_bf[b][:, cols], r[:], h_f32[b][:, cols], mult)
+
+        def update_gate(b, cols):
+            bank = matmul_piece(wzr_sb, b * P, x, cols)
+            nc.scalar.activation(z_f32[b][:, cols], bank[:], sigmoid)
+            one_minus_z = gates.tile([P, PIECE], F32, name="one_minus_z")
+            nc.scalar.activation(one_minus_z[:], bank[:], sigmoid, scale=-1.0)
+            product_engine[b].tensor_tensor(kept[b][:, cols], one_minus_z[:], h_f32[b][:, cols], mult)
+
+        def candidate(b, cols):
+            bank = matmul_piece(wt_sb, b * P, y, cols)
+            t = gates.tile([P, PIECE], F32, name="t")
+            nc.scalar.activation(t[:], bank[:], tanh)
+            product_engine[b].tensor_tensor(fresh[b][:, cols], z_f32[b][:, cols], t[:], mult)
+
+        def scatter_and_store(b):
+            nc.vector.tensor_tensor(window[b][:].indirect(offsets[:]), kept[b][:], fresh[b][:], add)
+            rows = slice(b * P, (b + 1) * P)
+            nc.sync.dma_start(out[rows, : S // 2], window[b][:, : S // 2])
+            nc.scalar.dma_start(out[rows, S // 2 :], window[b][:, S // 2 :])
+
+        pieces = [slice(n * PIECE, (n + 1) * PIECE) for n in range(NP)]
+
+        for cols in pieces:
+            for b in range(CB):
+                nc.vector.tensor_copy(h_bf[b][:, cols], h_f32[b][:, cols])
+                nc.gpsimd.tensor_copy(inp_bf[b][:, cols], inp_f32[b][:, cols])
+            for b in range(CB):
+                reset_gate(b, cols)
+            update_gate(0, cols)
+        for cols in pieces:
+            candidate(0, cols)
+        scatter_and_store(0)
+
+        for cols in pieces:
+            update_gate(1, cols)
+        for cols in pieces:
+            candidate(1, cols)
+        scatter_and_store(1)

@@ -91,7 +91,7 @@ def tile_graphnn_kernel(tc, base, h, inp, wzr, wt, offs, out):
             nc.vector.tensor_tensor(window[b][:].indirect(offsets[:]), kept[b][:], fresh[b][:], add)
             rows = slice(b * P, (b + 1) * P)
             nc.sync.dma_start(out[rows, : S // 2], window[b][:, : S // 2])
-            nc.scalar.dma_start(out[rows, S // 2 :], window[b][:, S // 2 :])
+            nc.sync.dma_start(out[rows, S // 2 :], window[b][:, S // 2 :])
 
         pieces = [slice(n * PIECE, (n + 1) * PIECE) for n in range(NP)]
 

@@ -21,7 +21,7 @@ def tile_graphnn_kernel(tc, base, h, inp, wzr, wt, offs, out):
 
     with (
         tc.tile_pool(name="held", bufs=1) as held,
-        tc.tile_pool(name="gates", bufs=4) as gates,
+        tc.tile_pool(name="ring", bufs=4) as ring,
         tc.psum_pool(name="psum", bufs=8) as psum,
     ):
         offsets = held.tile([P, N // 16], U16, name="offsets")
@@ -32,10 +32,12 @@ def tile_graphnn_kernel(tc, base, h, inp, wzr, wt, offs, out):
         wt_sb = held.tile([P, KB, C], BF16, name="wt_sb")
         nc.scalar.dma_start(wt_sb[:], wt.rearrange("(kb p) m -> p kb m", p=P))
 
+        pieces = [slice(n * PIECE, (n + 1) * PIECE) for n in range(NP)]
+        whole = slice(0, N)
+
         h_f32 = [held.tile([P, N], F32, name=f"h_f32_{b}") for b in range(CB)]
         inp_f32 = [held.tile([P, N], F32, name=f"inp_f32_{b}") for b in range(CB)]
-        for n in range(NP):
-            cols = slice(n * PIECE, (n + 1) * PIECE)
+        for cols in pieces:
             for b in range(CB):
                 rows = slice(b * P, (b + 1) * P)
                 nc.sync.dma_start(h_f32[b][:, cols], h[rows, cols])
@@ -48,13 +50,13 @@ def tile_graphnn_kernel(tc, base, h, inp, wzr, wt, offs, out):
         h_bf = [held.tile([P, N], BF16, name=f"h_bf_{b}") for b in range(CB)]
         inp_bf = [held.tile([P, N], BF16, name=f"inp_bf_{b}") for b in range(CB)]
         rh_bf = [held.tile([P, N], BF16, name=f"rh_bf_{b}") for b in range(CB)]
-        z_f32 = [held.tile([P, N], F32, name=f"z_f32_{b}") for b in range(CB)]
+        z = [held.tile([P, N], F32, name=f"z_{b}") for b in range(CB)]
+        one_minus_z = [held.tile([P, N], F32, name=f"one_minus_z_{b}") for b in range(CB)]
+        t = [held.tile([P, N], F32, name=f"t_{b}") for b in range(CB)]
         kept = [held.tile([P, N], F32, name=f"kept_{b}") for b in range(CB)]
         fresh = [held.tile([P, N], F32, name=f"fresh_{b}") for b in range(CB)]
         x = h_bf + inp_bf
         y = rh_bf + inp_bf
-
-        product_engine = (nc.vector, nc.gpsimd)
 
         def matmul_piece(weights, first_col, moving, cols):
             bank = psum.tile([P, PIECE], F32, name="bank")
@@ -70,22 +72,24 @@ def tile_graphnn_kernel(tc, base, h, inp, wzr, wt, offs, out):
 
         def reset_gate(b, cols):
             bank = matmul_piece(wzr_sb, C + b * P, x, cols)
-            r = gates.tile([P, PIECE], F32, name="r")
+            r = ring.tile([P, PIECE], F32, name="r")
             nc.scalar.activation(r[:], bank[:], sigmoid)
             nc.vector.tensor_tensor(rh_bf[b][:, cols], r[:], h_f32[b][:, cols], mult)
 
         def update_gate(b, cols):
             bank = matmul_piece(wzr_sb, b * P, x, cols)
-            nc.scalar.activation(z_f32[b][:, cols], bank[:], sigmoid)
-            one_minus_z = gates.tile([P, PIECE], F32, name="one_minus_z")
-            nc.scalar.activation(one_minus_z[:], bank[:], sigmoid, scale=-1.0)
-            product_engine[b].tensor_tensor(kept[b][:, cols], one_minus_z[:], h_f32[b][:, cols], mult)
+            nc.scalar.activation(z[b][:, cols], bank[:], sigmoid)
+            nc.scalar.activation(one_minus_z[b][:, cols], bank[:], sigmoid, scale=-1.0)
 
         def candidate(b, cols):
             bank = matmul_piece(wt_sb, b * P, y, cols)
-            t = gates.tile([P, PIECE], F32, name="t")
-            nc.scalar.activation(t[:], bank[:], tanh)
-            product_engine[b].tensor_tensor(fresh[b][:, cols], z_f32[b][:, cols], t[:], mult)
+            nc.scalar.activation(t[b][:, cols], bank[:], tanh)
+
+        def keep(b, cols):
+            nc.vector.tensor_tensor(kept[b][:, cols], one_minus_z[b][:, cols], h_f32[b][:, cols], mult)
+
+        def renew(b, cols):
+            nc.vector.tensor_tensor(fresh[b][:, cols], z[b][:, cols], t[b][:, cols], mult)
 
         def scatter_and_store(b):
             nc.vector.tensor_tensor(window[b][:].indirect(offsets[:]), kept[b][:], fresh[b][:], add)
@@ -93,21 +97,23 @@ def tile_graphnn_kernel(tc, base, h, inp, wzr, wt, offs, out):
             nc.sync.dma_start(out[rows, : S // 2], window[b][:, : S // 2])
             nc.sync.dma_start(out[rows, S // 2 :], window[b][:, S // 2 :])
 
-        pieces = [slice(n * PIECE, (n + 1) * PIECE) for n in range(NP)]
-
         for cols in pieces:
             for b in range(CB):
                 nc.vector.tensor_copy(h_bf[b][:, cols], h_f32[b][:, cols])
-                nc.gpsimd.tensor_copy(inp_bf[b][:, cols], inp_f32[b][:, cols])
+                nc.vector.tensor_copy(inp_bf[b][:, cols], inp_f32[b][:, cols])
             for b in range(CB):
                 reset_gate(b, cols)
             update_gate(0, cols)
+            keep(0, cols)
         for cols in pieces:
             candidate(0, cols)
+            renew(0, cols)
         scatter_and_store(0)
 
         for cols in pieces:
             update_gate(1, cols)
         for cols in pieces:
             candidate(1, cols)
+        keep(1, whole)
+        renew(1, whole)
         scatter_and_store(1)

@@ -6,7 +6,6 @@ CB = C // P
 KB = K // P
 PIECE = 512
 NP = N // PIECE
-K_ORDER = (2, 3, 0, 1)
 
 FLOPS = 2 * K * (K + C) * N
 
@@ -19,70 +18,68 @@ def tile_graphnn_kernel(tc, base, h, inp, wzr, wt, offs, out):
     tanh = mybir.ActivationFunctionType.Tanh
     mult, add = mybir.AluOpType.mult, mybir.AluOpType.add
 
+    pieces = [slice(n * PIECE, (n + 1) * PIECE) for n in range(NP)]
+    whole = slice(0, N)
+    block_rows = [slice(b * P, (b + 1) * P) for b in range(KB)]
+
     with (
         tc.tile_pool(name="held", bufs=1) as held,
         tc.tile_pool(name="ring", bufs=4) as ring,
         tc.psum_pool(name="psum", bufs=8) as psum,
     ):
-        offsets = held.tile([P, N // 16], U16, name="offsets")
-        nc.sync.dma_start(offsets[:], offs)
-
+        x_dram = [h[block_rows[0], :], h[block_rows[1], :], inp[block_rows[0], :], inp[block_rows[1], :]]
+        x_f32 = [held.tile([P, N], F32, name=f"x_f32_{kb}") for kb in range(KB)]
         wzr_sb = held.tile([P, KB, K], BF16, name="wzr_sb")
-        nc.sync.dma_start(wzr_sb[:], wzr.rearrange("(kb p) m -> p kb m", p=P))
         wt_sb = held.tile([P, KB, C], BF16, name="wt_sb")
-        nc.scalar.dma_start(wt_sb[:], wt.rearrange("(kb p) m -> p kb m", p=P))
-
-        pieces = [slice(n * PIECE, (n + 1) * PIECE) for n in range(NP)]
-        whole = slice(0, N)
-
-        h_f32 = [held.tile([P, N], F32, name=f"h_f32_{b}") for b in range(CB)]
-        inp_f32 = [held.tile([P, N], F32, name=f"inp_f32_{b}") for b in range(CB)]
-        for cols in pieces:
-            for b in range(CB):
-                rows = slice(b * P, (b + 1) * P)
-                nc.sync.dma_start(h_f32[b][:, cols], h[rows, cols])
-                nc.scalar.dma_start(inp_f32[b][:, cols], inp[rows, cols])
-
+        offsets = held.tile([P, N // 16], U16, name="offsets")
         window = [held.tile([P, S], F32, name=f"window_{b}") for b in range(CB)]
-        for b in range(CB):
-            nc.sync.dma_start(window[b][:], base[b * P : (b + 1) * P, :])
 
-        h_bf = [held.tile([P, N], BF16, name=f"h_bf_{b}") for b in range(CB)]
-        inp_bf = [held.tile([P, N], BF16, name=f"inp_bf_{b}") for b in range(CB)]
+        queues = (nc.sync, nc.scalar)
+        for kb in range(KB):
+            queues[kb % 2].dma_start(wzr_sb[:, kb, :], wzr[block_rows[kb], :])
+            queues[(kb + 1) % 2].dma_start(x_f32[kb][:, pieces[0]], x_dram[kb][:, pieces[0]])
+        for cols in pieces[1:]:
+            for kb in range(KB):
+                queues[kb % 2].dma_start(x_f32[kb][:, cols], x_dram[kb][:, cols])
+        nc.scalar.dma_start(wt_sb[:], wt.rearrange("(kb p) m -> p kb m", p=P))
+        nc.sync.dma_start(offsets[:], offs)
+        for b in range(CB):
+            queues[b].dma_start(window[b][:], base[block_rows[b], :])
+
+        x_bf = [held.tile([P, N], BF16, name=f"x_bf_{kb}") for kb in range(KB)]
         rh_bf = [held.tile([P, N], BF16, name=f"rh_bf_{b}") for b in range(CB)]
+        y_bf = rh_bf + x_bf[CB:]
+        h_f32 = x_f32[:CB]
         z = [held.tile([P, N], F32, name=f"z_{b}") for b in range(CB)]
         one_minus_z = [held.tile([P, N], F32, name=f"one_minus_z_{b}") for b in range(CB)]
         t = [held.tile([P, N], F32, name=f"t_{b}") for b in range(CB)]
         kept = [held.tile([P, N], F32, name=f"kept_{b}") for b in range(CB)]
         fresh = [held.tile([P, N], F32, name=f"fresh_{b}") for b in range(CB)]
-        x = h_bf + inp_bf
-        y = rh_bf + inp_bf
 
-        def matmul_piece(weights, first_col, moving, cols):
-            bank = psum.tile([P, PIECE], F32, name="bank")
-            for step, kb in enumerate(K_ORDER):
-                nc.tensor.matmul(
-                    bank[:],
-                    weights[:, kb, first_col : first_col + P],
-                    moving[kb][:, cols],
-                    start=(step == 0),
-                    stop=(step == KB - 1),
-                )
-            return bank
+        def matmul_piece(weights, first_cols, moving, k_order, cols):
+            banks = [psum.tile([P, PIECE], F32, name="bank") for c0 in first_cols]
+            for step, kb in enumerate(k_order):
+                for bank, c0 in zip(banks, first_cols):
+                    nc.tensor.matmul(
+                        bank[:],
+                        weights[:, kb, c0 : c0 + P],
+                        moving[kb][:, cols],
+                        start=(step == 0),
+                        stop=(step == KB - 1),
+                    )
+            return banks
 
-        def reset_gate(b, cols):
-            bank = matmul_piece(wzr_sb, C + b * P, x, cols)
+        def reset_gate(b, bank, cols):
             r = ring.tile([P, PIECE], F32, name="r")
             nc.scalar.activation(r[:], bank[:], sigmoid)
             nc.vector.tensor_tensor(rh_bf[b][:, cols], r[:], h_f32[b][:, cols], mult)
 
-        def update_gate(b, cols):
-            bank = matmul_piece(wzr_sb, b * P, x, cols)
+        def update_gate(b, bank, cols):
             nc.scalar.activation(z[b][:, cols], bank[:], sigmoid)
             nc.scalar.activation(one_minus_z[b][:, cols], bank[:], sigmoid, scale=-1.0)
 
         def candidate(b, cols):
-            bank = matmul_piece(wt_sb, b * P, y, cols)
+            (bank,) = matmul_piece(wt_sb, [b * P], y_bf, (2, 3, 0, 1), cols)
             nc.scalar.activation(t[b][:, cols], bank[:], tanh)
 
         def keep(b, cols):
@@ -93,17 +90,18 @@ def tile_graphnn_kernel(tc, base, h, inp, wzr, wt, offs, out):
 
         def scatter_and_store(b):
             nc.vector.tensor_tensor(window[b][:].indirect(offsets[:]), kept[b][:], fresh[b][:], add)
-            rows = slice(b * P, (b + 1) * P)
-            nc.sync.dma_start(out[rows, : S // 2], window[b][:, : S // 2])
-            nc.sync.dma_start(out[rows, S // 2 :], window[b][:, S // 2 :])
+            nc.sync.dma_start(out[block_rows[b], : S // 2], window[b][:, : S // 2])
+            nc.sync.dma_start(out[block_rows[b], S // 2 :], window[b][:, S // 2 :])
 
         for cols in pieces:
-            for b in range(CB):
-                nc.vector.tensor_copy(h_bf[b][:, cols], h_f32[b][:, cols])
-                nc.vector.tensor_copy(inp_bf[b][:, cols], inp_f32[b][:, cols])
-            for b in range(CB):
-                reset_gate(b, cols)
-            update_gate(0, cols)
+            for kb in range(KB):
+                nc.vector.tensor_copy(x_bf[kb][:, cols], x_f32[kb][:, cols])
+
+        for cols in pieces:
+            r0_bank, r1_bank, z0_bank = matmul_piece(wzr_sb, [C, C + P, 0], x_bf, range(KB), cols)
+            reset_gate(0, r0_bank, cols)
+            reset_gate(1, r1_bank, cols)
+            update_gate(0, z0_bank, cols)
             keep(0, cols)
         for cols in pieces:
             candidate(0, cols)
@@ -111,7 +109,8 @@ def tile_graphnn_kernel(tc, base, h, inp, wzr, wt, offs, out):
         scatter_and_store(0)
 
         for cols in pieces:
-            update_gate(1, cols)
+            (z1_bank,) = matmul_piece(wzr_sb, [P], x_bf, range(KB), cols)
+            update_gate(1, z1_bank, cols)
         for cols in pieces:
             candidate(1, cols)
         keep(1, whole)

@@ -6,6 +6,7 @@ CB = C // P
 KB = K // P
 PIECE = 512
 NP = N // PIECE
+WARM_UP = 6
 
 FLOPS = 2 * K * (K + C) * N
 
@@ -45,6 +46,12 @@ def tile_graphnn_kernel(tc, base, h, inp, wzr, wt, offs, out):
         nc.sync.dma_start(offsets[:], offs)
         for b in range(CB):
             queues[b].dma_start(window[b][:], base[block_rows[b], :])
+
+        zeros = held.tile([P, PIECE], BF16, name="zeros")
+        nc.vector.memset(zeros[:], 0.0)
+        unread_bank = psum.tile([P, PIECE], F32, name="bank")
+        for i in range(WARM_UP):
+            nc.tensor.matmul(unread_bank[:], zeros[:, :P], zeros[:], start=True, stop=True)
 
         x_bf = [held.tile([P, N], BF16, name=f"x_bf_{kb}") for kb in range(KB)]
         rh_bf = [held.tile([P, N], BF16, name=f"rh_bf_{b}") for b in range(CB)]

@@ -6,7 +6,6 @@ CB = C // P
 KB = K // P
 PIECE = 512
 NP = N // PIECE
-WARM_UP = 6
 
 FLOPS = 2 * K * (K + C) * N
 
@@ -45,13 +44,7 @@ def tile_graphnn_kernel(tc, base, h, inp, wzr, wt, offs, out):
         nc.scalar.dma_start(wt_sb[:], wt.rearrange("(kb p) m -> p kb m", p=P))
         nc.sync.dma_start(offsets[:], offs)
         for b in range(CB):
-            queues[b].dma_start(window[b][:], base[block_rows[b], :])
-
-        zeros = held.tile([P, PIECE], BF16, name="zeros")
-        nc.vector.memset(zeros[:], 0.0)
-        unread_bank = psum.tile([P, PIECE], F32, name="bank")
-        for i in range(WARM_UP):
-            nc.tensor.matmul(unread_bank[:], zeros[:, :P], zeros[:], start=True, stop=True)
+            nc.sync.dma_start(window[b][:], base[block_rows[b], :])
 
         x_bf = [held.tile([P, N], BF16, name=f"x_bf_{kb}") for kb in range(KB)]
         rh_bf = [held.tile([P, N], BF16, name=f"rh_bf_{b}") for b in range(CB)]

@@ -21,40 +21,55 @@ def tile_graphnn_kernel(tc, base, h, inp, wzr, wt, offs, out):
     pieces = [slice(n * PIECE, (n + 1) * PIECE) for n in range(NP)]
     whole = slice(0, N)
     block_rows = [slice(b * P, (b + 1) * P) for b in range(KB)]
+    h_blocks, inp_blocks = slice(0, CB), slice(CB, KB)
 
     with (
         tc.tile_pool(name="held", bufs=1) as held,
         tc.tile_pool(name="ring", bufs=4) as ring,
         tc.psum_pool(name="psum", bufs=8) as psum,
     ):
-        x_dram = [h[block_rows[0], :], h[block_rows[1], :], inp[block_rows[0], :], inp[block_rows[1], :]]
-        x_f32 = [held.tile([P, N], F32, name=f"x_f32_{kb}") for kb in range(KB)]
+        x_f32 = held.tile([P, KB, N], F32, name="x_f32")
+        x_bf = held.tile([P, KB, N], BF16, name="x_bf")
         wzr_sb = held.tile([P, KB, K], BF16, name="wzr_sb")
         wt_sb = held.tile([P, KB, C], BF16, name="wt_sb")
         offsets = held.tile([P, N // 16], U16, name="offsets")
         window = [held.tile([P, S], F32, name=f"window_{b}") for b in range(CB)]
 
+        h_dram = h.rearrange("(b p) n -> p b n", p=P)
+        inp_dram = inp.rearrange("(b p) n -> p b n", p=P)
+
+        def load_and_round(queue, blocks, dram, cols):
+            queue.dma_start(x_f32[:, blocks, cols], dram[:, :, cols])
+            nc.vector.tensor_copy(x_bf[:, blocks, cols], x_f32[:, blocks, cols])
+
         queues = (nc.sync, nc.scalar)
         for kb in range(KB):
+            dram = h_dram if kb < CB else inp_dram
+            b = kb % CB
             queues[kb % 2].dma_start(wzr_sb[:, kb, :], wzr[block_rows[kb], :])
-            queues[(kb + 1) % 2].dma_start(x_f32[kb][:, pieces[0]], x_dram[kb][:, pieces[0]])
-        for cols in pieces[1:]:
-            for kb in range(KB):
-                queues[kb % 2].dma_start(x_f32[kb][:, cols], x_dram[kb][:, cols])
-        nc.scalar.dma_start(wt_sb[:], wt.rearrange("(kb p) m -> p kb m", p=P))
+            load_and_round(queues[(kb + 1) % 2], slice(kb, kb + 1), dram[:, b : b + 1, :], pieces[0])
+        load_and_round(nc.sync, h_blocks, h_dram, pieces[1])
+        load_and_round(nc.sync, inp_blocks, inp_dram, pieces[1])
+        nc.sync.dma_start(wt_sb[:], wt.rearrange("(kb p) m -> p kb m", p=P))
+        for cols in pieces[2:]:
+            load_and_round(nc.sync, h_blocks, h_dram, cols)
+            load_and_round(nc.sync, inp_blocks, inp_dram, cols)
         nc.sync.dma_start(offsets[:], offs)
         for b in range(CB):
             nc.sync.dma_start(window[b][:], base[block_rows[b], :])
 
-        x_bf = [held.tile([P, N], BF16, name=f"x_bf_{kb}") for kb in range(KB)]
-        rh_bf = [held.tile([P, N], BF16, name=f"rh_bf_{b}") for b in range(CB)]
-        y_bf = rh_bf + x_bf[CB:]
-        h_f32 = x_f32[:CB]
+        rh_bf = held.tile([P, CB, N], BF16, name="rh_bf")
         z = [held.tile([P, N], F32, name=f"z_{b}") for b in range(CB)]
         one_minus_z = [held.tile([P, N], F32, name=f"one_minus_z_{b}") for b in range(CB)]
         t = [held.tile([P, N], F32, name=f"t_{b}") for b in range(CB)]
         kept = [held.tile([P, N], F32, name=f"kept_{b}") for b in range(CB)]
         fresh = [held.tile([P, N], F32, name=f"fresh_{b}") for b in range(CB)]
+
+        def x_block(kb, cols):
+            return x_bf[:, kb, cols]
+
+        def y_block(kb, cols):
+            return rh_bf[:, kb, cols] if kb < CB else x_bf[:, kb, cols]
 
         def matmul_piece(weights, first_cols, moving, k_order, cols):
             banks = [psum.tile([P, PIECE], F32, name="bank") for c0 in first_cols]
@@ -63,7 +78,7 @@ def tile_graphnn_kernel(tc, base, h, inp, wzr, wt, offs, out):
                     nc.tensor.matmul(
                         bank[:],
                         weights[:, kb, c0 : c0 + P],
-                        moving[kb][:, cols],
+                        moving(kb, cols),
                         start=(step == 0),
                         stop=(step == KB - 1),
                     )
@@ -72,18 +87,18 @@ def tile_graphnn_kernel(tc, base, h, inp, wzr, wt, offs, out):
         def reset_gate(b, bank, cols):
             r = ring.tile([P, PIECE], F32, name="r")
             nc.scalar.activation(r[:], bank[:], sigmoid)
-            nc.vector.tensor_tensor(rh_bf[b][:, cols], r[:], h_f32[b][:, cols], mult)
+            nc.vector.tensor_tensor(rh_bf[:, b, cols], r[:], x_f32[:, b, cols], mult)
 
         def update_gate(b, bank, cols):
             nc.scalar.activation(z[b][:, cols], bank[:], sigmoid)
             nc.scalar.activation(one_minus_z[b][:, cols], bank[:], sigmoid, scale=-1.0)
 
         def candidate(b, cols):
-            (bank,) = matmul_piece(wt_sb, [b * P], y_bf, (2, 3, 0, 1), cols)
+            (bank,) = matmul_piece(wt_sb, [b * P], y_block, (2, 3, 0, 1), cols)
             nc.scalar.activation(t[b][:, cols], bank[:], tanh)
 
         def keep(b, cols):
-            nc.vector.tensor_tensor(kept[b][:, cols], one_minus_z[b][:, cols], h_f32[b][:, cols], mult)
+            nc.vector.tensor_tensor(kept[b][:, cols], one_minus_z[b][:, cols], x_f32[:, b, cols], mult)
 
         def renew(b, cols):
             nc.vector.tensor_tensor(fresh[b][:, cols], z[b][:, cols], t[b][:, cols], mult)
@@ -93,23 +108,22 @@ def tile_graphnn_kernel(tc, base, h, inp, wzr, wt, offs, out):
             nc.sync.dma_start(out[block_rows[b], : S // 2], window[b][:, : S // 2])
             nc.sync.dma_start(out[block_rows[b], S // 2 :], window[b][:, S // 2 :])
 
-        for cols in pieces:
-            for kb in range(KB):
-                nc.vector.tensor_copy(x_bf[kb][:, cols], x_f32[kb][:, cols])
-
-        for cols in pieces:
-            r0_bank, r1_bank, z0_bank = matmul_piece(wzr_sb, [C, C + P, 0], x_bf, range(KB), cols)
-            reset_gate(0, r0_bank, cols)
-            reset_gate(1, r1_bank, cols)
-            update_gate(0, z0_bank, cols)
-            keep(0, cols)
-        for cols in pieces:
-            candidate(0, cols)
-            renew(0, cols)
+        for n in range(NP + 1):
+            if n < NP:
+                cols = pieces[n]
+                r0_bank, r1_bank, z0_bank = matmul_piece(wzr_sb, [C, C + P, 0], x_block, range(KB), cols)
+                reset_gate(0, r0_bank, cols)
+                reset_gate(1, r1_bank, cols)
+                update_gate(0, z0_bank, cols)
+                keep(0, cols)
+            if n >= 1:
+                cols = pieces[n - 1]
+                candidate(0, cols)
+                renew(0, cols)
         scatter_and_store(0)
 
         for cols in pieces:
-            (z1_bank,) = matmul_piece(wzr_sb, [P], x_bf, range(KB), cols)
+            (z1_bank,) = matmul_piece(wzr_sb, [P], x_block, range(KB), cols)
             update_gate(1, z1_bank, cols)
         for cols in pieces:
             candidate(1, cols)

@@ -65,6 +65,10 @@ def tile_graphnn_kernel(tc, base, h, inp, wzr, wt, offs, out):
         kept = [held.tile([P, N], F32, name=f"kept_{b}") for b in range(CB)]
         fresh = [held.tile([P, N], F32, name=f"fresh_{b}") for b in range(CB)]
 
+        def halves(cols):
+            middle = (cols.start + cols.stop) // 2
+            return [slice(cols.start, middle), slice(middle, cols.stop)]
+
         def x_block(kb, cols):
             return x_bf[:, kb, cols]
 
@@ -72,11 +76,12 @@ def tile_graphnn_kernel(tc, base, h, inp, wzr, wt, offs, out):
             return rh_bf[:, kb, cols] if kb < CB else x_bf[:, kb, cols]
 
         def matmul_piece(weights, first_cols, moving, k_order, cols):
-            banks = [psum.tile([P, PIECE], F32, name="bank") for c0 in first_cols]
-            for step, kb in enumerate(k_order):
-                for bank, c0 in zip(banks, first_cols):
+            width = cols.stop - cols.start
+            banks = [psum.tile([P, PIECE], F32, name="bank")[:, :width] for c0 in first_cols]
+            for bank, c0 in zip(banks, first_cols):
+                for step, kb in enumerate(k_order):
                     nc.tensor.matmul(
-                        bank[:],
+                        bank,
                         weights[:, kb, c0 : c0 + P],
                         moving(kb, cols),
                         start=(step == 0),
@@ -86,16 +91,16 @@ def tile_graphnn_kernel(tc, base, h, inp, wzr, wt, offs, out):
 
         def reset_gate(b, bank, cols):
             r = ring.tile([P, PIECE], F32, name="r")
-            nc.scalar.activation(r[:], bank[:], sigmoid)
+            nc.scalar.activation(r[:], bank, sigmoid)
             nc.vector.tensor_tensor(rh_bf[:, b, cols], r[:], x_f32[:, b, cols], mult)
 
         def update_gate(b, bank, cols):
-            nc.scalar.activation(z[b][:, cols], bank[:], sigmoid)
-            nc.scalar.activation(one_minus_z[b][:, cols], bank[:], sigmoid, scale=-1.0)
+            nc.scalar.activation(z[b][:, cols], bank, sigmoid)
+            nc.scalar.activation(one_minus_z[b][:, cols], bank, sigmoid, scale=-1.0)
 
         def candidate(b, cols):
             (bank,) = matmul_piece(wt_sb, [b * P], y_block, (2, 3, 0, 1), cols)
-            nc.scalar.activation(t[b][:, cols], bank[:], tanh)
+            nc.scalar.activation(t[b][:, cols], bank, tanh)
 
         def keep(b, cols):
             nc.vector.tensor_tensor(kept[b][:, cols], one_minus_z[b][:, cols], x_f32[:, b, cols], mult)
@@ -117,9 +122,9 @@ def tile_graphnn_kernel(tc, base, h, inp, wzr, wt, offs, out):
                 update_gate(0, z0_bank, cols)
                 keep(0, cols)
             if n >= 1:
-                cols = pieces[n - 1]
-                candidate(0, cols)
-                renew(0, cols)
+                for cols in halves(pieces[n - 1]) if n == NP else [pieces[n - 1]]:
+                    candidate(0, cols)
+                    renew(0, cols)
         scatter_and_store(0)
 
         for cols in pieces:

@@ -1,4 +1,5 @@
 import concourse.mybir as mybir
+from concourse.masks import make_identity
 
 P = 128
 C, K, S, N = 256, 512, 4096, 2048
@@ -34,6 +35,8 @@ def tile_graphnn_kernel(tc, base, h, inp, wzr, wt, offs, out):
         wt_sb = held.tile([P, KB, C], BF16, name="wt_sb")
         offsets = held.tile([P, N // 16], U16, name="offsets")
         window = [held.tile([P, S], F32, name=f"window_{b}") for b in range(CB)]
+        identity = held.tile([P, P], F32, name="identity")
+        make_identity(nc, identity[:])
 
         h_dram = h.rearrange("(b p) n -> p b n", p=P)
         inp_dram = inp.rearrange("(b p) n -> p b n", p=P)
@@ -132,6 +135,12 @@ def tile_graphnn_kernel(tc, base, h, inp, wzr, wt, offs, out):
             update_gate(1, z1_bank, cols)
         for cols in pieces:
             candidate(1, cols)
-        keep(1, whole)
-        renew(1, whole)
+        h1_banks = [psum.tile([P, PIECE], F32, name="bank") for cols in pieces]
+        for h1_bank, cols in zip(h1_banks, pieces):
+            nc.tensor.matmul(h1_bank[:], identity[:], x_f32[:, 1, cols], start=True, stop=True)
+        first_half, second_half = halves(whole)
+        nc.gpsimd.tensor_tensor(fresh[1][:, first_half], z[1][:, first_half], t[1][:, first_half], mult)
+        for h1_bank, cols in zip(h1_banks, pieces):
+            nc.vector.tensor_tensor(kept[1][:, cols], one_minus_z[1][:, cols], h1_bank[:], mult)
+        renew(1, second_half)
         scatter_and_store(1)

@@ -78,18 +78,23 @@ def tile_graphnn_kernel(tc, base, h, inp, wzr, wt, offs, out):
         def y_block(kb, cols):
             return rh_bf[:, kb, cols] if kb < CB else x_bf[:, kb, cols]
 
-        def matmul_piece(weights, first_cols, moving, k_order, cols):
+        def matmul_piece(weights, first_cols, moving, k_order, cols, bank_by_bank=True):
             width = cols.stop - cols.start
             banks = [psum.tile([P, PIECE], F32, name="bank")[:, :width] for c0 in first_cols]
-            for bank, c0 in zip(banks, first_cols):
-                for step, kb in enumerate(k_order):
-                    nc.tensor.matmul(
-                        bank,
-                        weights[:, kb, c0 : c0 + P],
-                        moving(kb, cols),
-                        start=(step == 0),
-                        stop=(step == KB - 1),
-                    )
+            steps = list(enumerate(k_order))
+            outputs = list(zip(banks, first_cols))
+            if bank_by_bank:
+                order = [(output, step) for output in outputs for step in steps]
+            else:
+                order = [(output, step) for step in steps for output in outputs]
+            for (bank, c0), (step, kb) in order:
+                nc.tensor.matmul(
+                    bank,
+                    weights[:, kb, c0 : c0 + P],
+                    moving(kb, cols),
+                    start=(step == 0),
+                    stop=(step == KB - 1),
+                )
             return banks
 
         def reset_gate(b, bank, cols):
@@ -119,7 +124,9 @@ def tile_graphnn_kernel(tc, base, h, inp, wzr, wt, offs, out):
         for n in range(NP + 1):
             if n < NP:
                 cols = pieces[n]
-                r0_bank, r1_bank, z0_bank = matmul_piece(wzr_sb, [C, C + P, 0], x_block, range(KB), cols)
+                r0_bank, r1_bank, z0_bank = matmul_piece(
+                    wzr_sb, [C, C + P, 0], x_block, range(KB), cols, bank_by_bank=(n == NP - 1)
+                )
                 reset_gate(0, r0_bank, cols)
                 reset_gate(1, r1_bank, cols)
                 update_gate(0, z0_bank, cols)

@@ -20,7 +20,6 @@ def tile_graphnn_kernel(tc, base, h, inp, wzr, wt, offs, out):
     mult, add = mybir.AluOpType.mult, mybir.AluOpType.add
 
     pieces = [slice(n * PIECE, (n + 1) * PIECE) for n in range(NP)]
-    whole = slice(0, N)
     block_rows = [slice(b * P, (b + 1) * P) for b in range(KB)]
     h_blocks, inp_blocks = slice(0, CB), slice(CB, KB)
 
@@ -49,8 +48,8 @@ def tile_graphnn_kernel(tc, base, h, inp, wzr, wt, offs, out):
         for kb in range(KB):
             dram = h_dram if kb < CB else inp_dram
             b = kb % CB
-            queues[kb % 2].dma_start(wzr_sb[:, kb, :], wzr[block_rows[kb], :])
-            load_and_round(queues[(kb + 1) % 2], slice(kb, kb + 1), dram[:, b : b + 1, :], pieces[0])
+            load_and_round(queues[kb % 2], slice(kb, kb + 1), dram[:, b : b + 1, :], pieces[0])
+            queues[(kb + 1) % 2].dma_start(wzr_sb[:, kb, :], wzr[block_rows[kb], :])
         load_and_round(nc.sync, h_blocks, h_dram, pieces[1])
         load_and_round(nc.sync, inp_blocks, inp_dram, pieces[1])
         nc.sync.dma_start(wt_sb[:], wt.rearrange("(kb p) m -> p kb m", p=P))
@@ -142,12 +141,20 @@ def tile_graphnn_kernel(tc, base, h, inp, wzr, wt, offs, out):
             update_gate(1, z1_bank, cols)
         for cols in pieces:
             candidate(1, cols)
-        h1_banks = [psum.tile([P, PIECE], F32, name="bank") for cols in pieces]
+        def in_psum(source):
+            width = source.shape[-1]
+            bank = psum.tile([P, PIECE], F32, name="bank")[:, :width]
+            nc.tensor.matmul(bank, identity[:], source, start=True, stop=True)
+            return bank
+
+        gpsimd_cols = -(-2 * N // (3 * P)) * P
+        gpsimd_part = slice(0, gpsimd_cols)
+        vector_parts = [slice(c, min(c + PIECE, N)) for c in range(gpsimd_cols, N, PIECE)]
+        h1_banks = [in_psum(x_f32[:, 1, cols]) for cols in pieces]
+        z1_banks = [in_psum(z[1][:, cols]) for cols in vector_parts]
+        nc.gpsimd.tensor_tensor(fresh[1][:, gpsimd_part], z[1][:, gpsimd_part], t[1][:, gpsimd_part], mult)
         for h1_bank, cols in zip(h1_banks, pieces):
-            nc.tensor.matmul(h1_bank[:], identity[:], x_f32[:, 1, cols], start=True, stop=True)
-        first_half, second_half = halves(whole)
-        nc.gpsimd.tensor_tensor(fresh[1][:, first_half], z[1][:, first_half], t[1][:, first_half], mult)
-        for h1_bank, cols in zip(h1_banks, pieces):
-            nc.vector.tensor_tensor(kept[1][:, cols], one_minus_z[1][:, cols], h1_bank[:], mult)
-        renew(1, second_half)
+            nc.vector.tensor_tensor(kept[1][:, cols], one_minus_z[1][:, cols], h1_bank, mult)
+        for z1_bank, cols in zip(z1_banks, vector_parts):
+            nc.vector.tensor_tensor(fresh[1][:, cols], t[1][:, cols], z1_bank, mult)
         scatter_and_store(1)

@@ -50,8 +50,9 @@ def tile_graphnn_kernel(tc, base, h, inp, wzr, wt, offs, out):
             b = kb % CB
             load_and_round(queues[kb % 2], slice(kb, kb + 1), dram[:, b : b + 1, :], pieces[0])
             queues[(kb + 1) % 2].dma_start(wzr_sb[:, kb, :], wzr[block_rows[kb], :])
-        load_and_round(nc.sync, h_blocks, h_dram, pieces[1])
-        load_and_round(nc.sync, inp_blocks, inp_dram, pieces[1])
+        for kb in range(KB):
+            dram = h_dram if kb < CB else inp_dram
+            load_and_round(nc.sync, slice(kb, kb + 1), dram[:, kb % CB : kb % CB + 1, :], pieces[1])
         nc.sync.dma_start(wt_sb[:], wt.rearrange("(kb p) m -> p kb m", p=P))
         for cols in pieces[2:]:
             load_and_round(nc.sync, h_blocks, h_dram, cols)

@@ -40,23 +40,20 @@ def tile_graphnn_kernel(tc, base, h, inp, wzr, wt, offs, out):
         h_dram = h.rearrange("(b p) n -> p b n", p=P)
         inp_dram = inp.rearrange("(b p) n -> p b n", p=P)
 
-        def load_and_round(queue, blocks, dram, cols):
-            queue.dma_start(x_f32[:, blocks, cols], dram[:, :, cols])
+        def load_and_round(blocks, dram, cols):
+            nc.sync.dma_start(x_f32[:, blocks, cols], dram[:, :, cols])
             nc.vector.tensor_copy(x_bf[:, blocks, cols], x_f32[:, blocks, cols])
 
-        queues = (nc.sync, nc.scalar)
-        for kb in range(KB):
-            dram = h_dram if kb < CB else inp_dram
-            b = kb % CB
-            load_and_round(queues[kb % 2], slice(kb, kb + 1), dram[:, b : b + 1, :], pieces[0])
-            queues[(kb + 1) % 2].dma_start(wzr_sb[:, kb, :], wzr[block_rows[kb], :])
-        for kb in range(KB):
-            dram = h_dram if kb < CB else inp_dram
-            load_and_round(nc.sync, slice(kb, kb + 1), dram[:, kb % CB : kb % CB + 1, :], pieces[1])
+        for cols in pieces[:2]:
+            for kb in range(KB):
+                dram = h_dram if kb < CB else inp_dram
+                load_and_round(slice(kb, kb + 1), dram[:, kb % CB : kb % CB + 1, :], cols)
+                if cols == pieces[0]:
+                    nc.sync.dma_start(wzr_sb[:, kb, :], wzr[block_rows[kb], :])
         nc.sync.dma_start(wt_sb[:], wt.rearrange("(kb p) m -> p kb m", p=P))
         for cols in pieces[2:]:
-            load_and_round(nc.sync, h_blocks, h_dram, cols)
-            load_and_round(nc.sync, inp_blocks, inp_dram, cols)
+            load_and_round(h_blocks, h_dram, cols)
+            load_and_round(inp_blocks, inp_dram, cols)
         nc.sync.dma_start(offsets[:], offs)
         for b in range(CB):
             nc.sync.dma_start(window[b][:], base[block_rows[b], :])

@@ -40,16 +40,26 @@ def tile_graphnn_kernel(tc, base, h, inp, wzr, wt, offs, out):
         h_dram = h.rearrange("(b p) n -> p b n", p=P)
         inp_dram = inp.rearrange("(b p) n -> p b n", p=P)
 
+        def halves(cols):
+            middle = (cols.start + cols.stop) // 2
+            return [slice(cols.start, middle), slice(middle, cols.stop)]
+
         def load_and_round(blocks, dram, cols):
             nc.sync.dma_start(x_f32[:, blocks, cols], dram[:, :, cols])
             nc.vector.tensor_copy(x_bf[:, blocks, cols], x_f32[:, blocks, cols])
 
-        for cols in pieces[:2]:
-            for kb in range(KB):
-                dram = h_dram if kb < CB else inp_dram
-                load_and_round(slice(kb, kb + 1), dram[:, kb % CB : kb % CB + 1, :], cols)
-                if cols == pieces[0]:
-                    nc.sync.dma_start(wzr_sb[:, kb, :], wzr[block_rows[kb], :])
+        def load_block(kb, cols):
+            dram = h_dram if kb < CB else inp_dram
+            load_and_round(slice(kb, kb + 1), dram[:, kb % CB : kb % CB + 1, :], cols)
+
+        for kb in range(KB):
+            parts = halves(pieces[0]) if kb == 0 else [pieces[0]]
+            load_block(kb, parts[0])
+            nc.sync.dma_start(wzr_sb[:, kb, :], wzr[block_rows[kb], :])
+            for cols in parts[1:]:
+                load_block(kb, cols)
+        for kb in range(KB):
+            load_block(kb, pieces[1])
         nc.sync.dma_start(wt_sb[:], wt.rearrange("(kb p) m -> p kb m", p=P))
         for cols in pieces[2:]:
             load_and_round(h_blocks, h_dram, cols)
@@ -65,26 +75,21 @@ def tile_graphnn_kernel(tc, base, h, inp, wzr, wt, offs, out):
         kept = [held.tile([P, N], F32, name=f"kept_{b}") for b in range(CB)]
         fresh = [held.tile([P, N], F32, name=f"fresh_{b}") for b in range(CB)]
 
-        def halves(cols):
-            middle = (cols.start + cols.stop) // 2
-            return [slice(cols.start, middle), slice(middle, cols.stop)]
-
         def x_block(kb, cols):
             return x_bf[:, kb, cols]
 
         def y_block(kb, cols):
             return rh_bf[:, kb, cols] if kb < CB else x_bf[:, kb, cols]
 
-        def matmul_piece(weights, first_cols, moving, k_order, cols, bank_by_bank=True):
-            width = cols.stop - cols.start
-            banks = [psum.tile([P, PIECE], F32, name="bank")[:, :width] for c0 in first_cols]
+        def matmul_group(weights, outputs, moving, k_order, bank_by_bank=True):
+            banks = [psum.tile([P, PIECE], F32, name="bank")[:, : cols.stop - cols.start] for c0, cols in outputs]
             steps = list(enumerate(k_order))
-            outputs = list(zip(banks, first_cols))
+            targets = list(zip(banks, outputs))
             if bank_by_bank:
-                order = [(output, step) for output in outputs for step in steps]
+                order = [(target, step) for target in targets for step in steps]
             else:
-                order = [(output, step) for step in steps for output in outputs]
-            for (bank, c0), (step, kb) in order:
+                order = [(target, step) for step in steps for target in targets]
+            for (bank, (c0, cols)), (step, kb) in order:
                 nc.tensor.matmul(
                     bank,
                     weights[:, kb, c0 : c0 + P],
@@ -95,16 +100,16 @@ def tile_graphnn_kernel(tc, base, h, inp, wzr, wt, offs, out):
             return banks
 
         def reset_gate(b, bank, cols):
-            r = ring.tile([P, PIECE], F32, name="r")
-            nc.scalar.activation(r[:], bank, sigmoid)
-            nc.vector.tensor_tensor(rh_bf[:, b, cols], r[:], x_f32[:, b, cols], mult)
+            r = ring.tile([P, PIECE], F32, name="r")[:, : cols.stop - cols.start]
+            nc.scalar.activation(r, bank, sigmoid)
+            nc.vector.tensor_tensor(rh_bf[:, b, cols], r, x_f32[:, b, cols], mult)
 
         def update_gate(b, bank, cols):
             nc.scalar.activation(z[b][:, cols], bank, sigmoid)
             nc.scalar.activation(one_minus_z[b][:, cols], bank, sigmoid, scale=-1.0)
 
         def candidate(b, cols):
-            (bank,) = matmul_piece(wt_sb, [b * P], y_block, (2, 3, 0, 1), cols)
+            (bank,) = matmul_group(wt_sb, [(b * P, cols)], y_block, (2, 3, 0, 1))
             nc.scalar.activation(t[b][:, cols], bank, tanh)
 
         def keep(b, cols):
@@ -120,14 +125,15 @@ def tile_graphnn_kernel(tc, base, h, inp, wzr, wt, offs, out):
 
         for n in range(NP + 1):
             if n < NP:
-                cols = pieces[n]
-                r0_bank, r1_bank, z0_bank = matmul_piece(
-                    wzr_sb, [C, C + P, 0], x_block, range(KB), cols, bank_by_bank=(n == NP - 1)
-                )
-                reset_gate(0, r0_bank, cols)
-                reset_gate(1, r1_bank, cols)
-                update_gate(0, z0_bank, cols)
-                keep(0, cols)
+                parts = halves(pieces[0]) if n == 0 else [pieces[n]]
+                gates = [(c0, cols) for cols in parts for c0 in (C, C + P, 0)]
+                banks = matmul_group(wzr_sb, gates, x_block, range(KB), bank_by_bank=(n == NP - 1))
+                for i, cols in enumerate(parts):
+                    r0_bank, r1_bank, z0_bank = banks[3 * i : 3 * i + 3]
+                    reset_gate(0, r0_bank, cols)
+                    reset_gate(1, r1_bank, cols)
+                    update_gate(0, z0_bank, cols)
+                    keep(0, cols)
             if n >= 1:
                 for cols in halves(pieces[n - 1]) if n == NP else [pieces[n - 1]]:
                     candidate(0, cols)
@@ -135,7 +141,7 @@ def tile_graphnn_kernel(tc, base, h, inp, wzr, wt, offs, out):
         scatter_and_store(0)
 
         for cols in pieces:
-            (z1_bank,) = matmul_piece(wzr_sb, [P], x_block, range(KB), cols)
+            (z1_bank,) = matmul_group(wzr_sb, [(P, cols)], x_block, range(KB))
             update_gate(1, z1_bank, cols)
         for cols in pieces:
             candidate(1, cols)

@@ -99,10 +99,12 @@ def tile_graphnn_kernel(tc, base, h, inp, wzr, wt, offs, out):
                 )
             return banks
 
-        def reset_gate(b, bank, cols):
-            r = ring.tile([P, PIECE], F32, name="r")[:, : cols.stop - cols.start]
-            nc.scalar.activation(r, bank, sigmoid)
-            nc.vector.tensor_tensor(rh_bf[:, b, cols], r, x_f32[:, b, cols], mult)
+        def reset_gate(b, banks, parts):
+            piece = slice(parts[0].start, parts[-1].stop)
+            r = ring.tile([P, PIECE], F32, name="r")
+            for bank, cols in zip(banks, parts):
+                nc.scalar.activation(r[:, cols.start - piece.start : cols.stop - piece.start], bank, sigmoid)
+            nc.vector.tensor_tensor(rh_bf[:, b, piece], r[:], x_f32[:, b, piece], mult)
 
         def update_gate(b, bank, cols):
             nc.scalar.activation(z[b][:, cols], bank, sigmoid)
@@ -128,12 +130,12 @@ def tile_graphnn_kernel(tc, base, h, inp, wzr, wt, offs, out):
                 parts = halves(pieces[0]) if n == 0 else [pieces[n]]
                 gates = [(c0, cols) for cols in parts for c0 in (C, C + P, 0)]
                 banks = matmul_group(wzr_sb, gates, x_block, range(KB), bank_by_bank=(n == NP - 1))
-                for i, cols in enumerate(parts):
-                    r0_bank, r1_bank, z0_bank = banks[3 * i : 3 * i + 3]
-                    reset_gate(0, r0_bank, cols)
-                    reset_gate(1, r1_bank, cols)
+                r0_banks, r1_banks, z0_banks = [banks[gate::3] for gate in range(3)]
+                reset_gate(0, r0_banks, parts)
+                reset_gate(1, r1_banks, parts)
+                for z0_bank, cols in zip(z0_banks, parts):
                     update_gate(0, z0_bank, cols)
-                    keep(0, cols)
+                keep(0, pieces[n])
             if n >= 1:
                 for cols in halves(pieces[n - 1]) if n == NP else [pieces[n - 1]]:
                     candidate(0, cols)

@@ -107,8 +107,8 @@ def tile_graphnn_kernel(tc, base, h, inp, wzr, wt, offs, out):
             nc.vector.tensor_tensor(rh_bf[:, b, piece], r[:], x_f32[:, b, piece], mult)
 
         def update_gate(b, bank, cols):
-            nc.scalar.activation(z[b][:, cols], bank, sigmoid)
             nc.scalar.activation(one_minus_z[b][:, cols], bank, sigmoid, scale=-1.0)
+            nc.scalar.activation(z[b][:, cols], bank, sigmoid)
 
         def candidate(b, cols):
             (bank,) = matmul_group(wt_sb, [(b * P, cols)], y_block, (2, 3, 0, 1))
@@ -122,8 +122,7 @@ def tile_graphnn_kernel(tc, base, h, inp, wzr, wt, offs, out):
 
         def scatter_and_store(b):
             nc.vector.tensor_tensor(window[b][:].indirect(offsets[:]), kept[b][:], fresh[b][:], add)
-            nc.sync.dma_start(out[block_rows[b], : S // 2], window[b][:, : S // 2])
-            nc.sync.dma_start(out[block_rows[b], S // 2 :], window[b][:, S // 2 :])
+            nc.sync.dma_start(out[block_rows[b], :], window[b][:])
 
         for n in range(NP + 1):
             if n < NP:
@@ -137,7 +136,12 @@ def tile_graphnn_kernel(tc, base, h, inp, wzr, wt, offs, out):
                     update_gate(0, z0_bank, cols)
                 keep(0, pieces[n])
             if n >= 1:
-                for cols in halves(pieces[n - 1]) if n == NP else [pieces[n - 1]]:
+                t_parts = [pieces[n - 1]]
+                if n >= NP - 1:
+                    t_parts = halves(pieces[n - 1])
+                if n == NP:
+                    t_parts = t_parts[:1] + halves(t_parts[1])
+                for cols in t_parts:
                     candidate(0, cols)
                     renew(0, cols)
         scatter_and_store(0)

@@ -54,10 +54,13 @@ def tile_graphnn_kernel(tc, base, h, inp, wzr, wt, offs, out):
 
         for kb in range(KB):
             parts = halves(pieces[0]) if kb == 0 else [pieces[0]]
+            gate_cols = [slice(C, K), slice(0, C)] if kb == 0 else [slice(0, K)]
             load_block(kb, parts[0])
-            nc.sync.dma_start(wzr_sb[:, kb, :], wzr[block_rows[kb], :])
+            nc.sync.dma_start(wzr_sb[:, kb, gate_cols[0]], wzr[block_rows[kb], gate_cols[0]])
             for cols in parts[1:]:
                 load_block(kb, cols)
+            for c_cols in gate_cols[1:]:
+                nc.sync.dma_start(wzr_sb[:, kb, c_cols], wzr[block_rows[kb], c_cols])
         for kb in range(KB):
             load_block(kb, pieces[1])
         nc.sync.dma_start(wt_sb[:], wt.rearrange("(kb p) m -> p kb m", p=P))
@@ -127,9 +130,10 @@ def tile_graphnn_kernel(tc, base, h, inp, wzr, wt, offs, out):
         for n in range(NP + 1):
             if n < NP:
                 parts = halves(pieces[0]) if n == 0 else [pieces[n]]
-                gates = [(c0, cols) for cols in parts for c0 in (C, C + P, 0)]
+                gates = [(c0, cols) for cols in parts for c0 in (C, C + P)] + [(0, cols) for cols in parts]
                 banks = matmul_group(wzr_sb, gates, x_block, range(KB), bank_by_bank=(n == NP - 1))
-                r0_banks, r1_banks, z0_banks = [banks[gate::3] for gate in range(3)]
+                z0_banks = banks[2 * len(parts) :]
+                r0_banks, r1_banks = [banks[b : 2 * len(parts) : 2] for b in range(CB)]
                 reset_gate(0, r0_banks, parts)
                 reset_gate(1, r1_banks, parts)
                 for z0_bank, cols in zip(z0_banks, parts):

import concourse.mybir as mybir
from concourse.masks import make_identity

P = 128
C, K, S, N = 256, 512, 4096, 2048
CB = C // P
KB = K // P
PIECE = 512
NP = N // PIECE

FLOPS = 2 * K * (K + C) * N

F32, BF16, U16 = mybir.dt.float32, mybir.dt.bfloat16, mybir.dt.uint16


def tile_graphnn_kernel(tc, base, h, inp, wzr, wt, offs, out):
    nc = tc.nc
    sigmoid = mybir.ActivationFunctionType.Sigmoid
    tanh = mybir.ActivationFunctionType.Tanh
    mult, add = mybir.AluOpType.mult, mybir.AluOpType.add

    pieces = [slice(n * PIECE, (n + 1) * PIECE) for n in range(NP)]
    block_rows = [slice(b * P, (b + 1) * P) for b in range(KB)]
    h_blocks, inp_blocks = slice(0, CB), slice(CB, KB)

    with (
        tc.tile_pool(name="held", bufs=1) as held,
        tc.tile_pool(name="ring", bufs=4) as ring,
        tc.psum_pool(name="psum", bufs=8) as psum,
    ):
        x_f32 = held.tile([P, KB, N], F32, name="x_f32")
        x_bf = held.tile([P, KB, N], BF16, name="x_bf")
        wzr_sb = held.tile([P, KB, K], BF16, name="wzr_sb")
        wt_sb = held.tile([P, KB, C], BF16, name="wt_sb")
        offsets = held.tile([P, N // 16], U16, name="offsets")
        window = [held.tile([P, S], F32, name=f"window_{b}") for b in range(CB)]
        identity = held.tile([P, P], F32, name="identity")
        make_identity(nc, identity[:])

        h_dram = h.rearrange("(b p) n -> p b n", p=P)
        inp_dram = inp.rearrange("(b p) n -> p b n", p=P)

        def halves(cols):
            middle = (cols.start + cols.stop) // 2
            return [slice(cols.start, middle), slice(middle, cols.stop)]

        def load_and_round(blocks, dram, cols):
            nc.sync.dma_start(x_f32[:, blocks, cols], dram[:, :, cols])
            nc.vector.tensor_copy(x_bf[:, blocks, cols], x_f32[:, blocks, cols])

        def load_block(kb, cols):
            dram = h_dram if kb < CB else inp_dram
            load_and_round(slice(kb, kb + 1), dram[:, kb % CB : kb % CB + 1, :], cols)

        for kb in range(KB):
            parts = halves(pieces[0]) if kb == 0 else [pieces[0]]
            gate_cols = [slice(C, K), slice(0, C)] if kb == 0 else [slice(0, K)]
            load_block(kb, parts[0])
            nc.sync.dma_start(wzr_sb[:, kb, gate_cols[0]], wzr[block_rows[kb], gate_cols[0]])
            for cols in parts[1:]:
                load_block(kb, cols)
            for c_cols in gate_cols[1:]:
                nc.sync.dma_start(wzr_sb[:, kb, c_cols], wzr[block_rows[kb], c_cols])
        for kb in range(KB):
            load_block(kb, pieces[1])
        nc.sync.dma_start(wt_sb[:], wt.rearrange("(kb p) m -> p kb m", p=P))
        for cols in pieces[2:]:
            load_and_round(h_blocks, h_dram, cols)
            load_and_round(inp_blocks, inp_dram, cols)
        nc.sync.dma_start(offsets[:], offs)
        for b in range(CB):
            nc.sync.dma_start(window[b][:], base[block_rows[b], :])

        rh_bf = held.tile([P, CB, N], BF16, name="rh_bf")
        z = [held.tile([P, N], F32, name=f"z_{b}") for b in range(CB)]
        one_minus_z = [held.tile([P, N], F32, name=f"one_minus_z_{b}") for b in range(CB)]
        t = [held.tile([P, N], F32, name=f"t_{b}") for b in range(CB)]
        kept = [held.tile([P, N], F32, name=f"kept_{b}") for b in range(CB)]
        fresh = [held.tile([P, N], F32, name=f"fresh_{b}") for b in range(CB)]

        def x_block(kb, cols):
            return x_bf[:, kb, cols]

        def y_block(kb, cols):
            return rh_bf[:, kb, cols] if kb < CB else x_bf[:, kb, cols]

        def matmul_group(weights, outputs, moving, k_order, bank_by_bank=True):
            banks = [psum.tile([P, PIECE], F32, name="bank")[:, : cols.stop - cols.start] for c0, cols in outputs]
            steps = list(enumerate(k_order))
            targets = list(zip(banks, outputs))
            if bank_by_bank:
                order = [(target, step) for target in targets for step in steps]
            else:
                order = [(target, step) for step in steps for target in targets]
            for (bank, (c0, cols)), (step, kb) in order:
                nc.tensor.matmul(
                    bank,
                    weights[:, kb, c0 : c0 + P],
                    moving(kb, cols),
                    start=(step == 0),
                    stop=(step == KB - 1),
                )
            return banks

        def reset_gate(b, banks, parts):
            piece = slice(parts[0].start, parts[-1].stop)
            r = ring.tile([P, PIECE], F32, name="r")
            for bank, cols in zip(banks, parts):
                nc.scalar.activation(r[:, cols.start - piece.start : cols.stop - piece.start], bank, sigmoid)
            nc.vector.tensor_tensor(rh_bf[:, b, piece], r[:], x_f32[:, b, piece], mult)

        def update_gate(b, bank, cols):
            nc.scalar.activation(one_minus_z[b][:, cols], bank, sigmoid, scale=-1.0)
            nc.scalar.activation(z[b][:, cols], bank, sigmoid)

        def candidate(b, cols):
            (bank,) = matmul_group(wt_sb, [(b * P, cols)], y_block, (2, 3, 0, 1))
            nc.scalar.activation(t[b][:, cols], bank, tanh)

        def keep(b, cols):
            nc.vector.tensor_tensor(kept[b][:, cols], one_minus_z[b][:, cols], x_f32[:, b, cols], mult)

        def renew(b, cols):
            nc.vector.tensor_tensor(fresh[b][:, cols], z[b][:, cols], t[b][:, cols], mult)

        def scatter_and_store(b):
            nc.vector.tensor_tensor(window[b][:].indirect(offsets[:]), kept[b][:], fresh[b][:], add)
            nc.sync.dma_start(out[block_rows[b], :], window[b][:])

        for n in range(NP + 1):
            if n < NP:
                parts = halves(pieces[0]) if n == 0 else [pieces[n]]
                gates = [(c0, cols) for cols in parts for c0 in (C, C + P)] + [(0, cols) for cols in parts]
                banks = matmul_group(wzr_sb, gates, x_block, range(KB), bank_by_bank=(n == NP - 1))
                z0_banks = banks[2 * len(parts) :]
                r0_banks, r1_banks = [banks[b : 2 * len(parts) : 2] for b in range(CB)]
                reset_gate(0, r0_banks, parts)
                reset_gate(1, r1_banks, parts)
                for z0_bank, cols in zip(z0_banks, parts):
                    update_gate(0, z0_bank, cols)
                keep(0, pieces[n])
            if n >= 1:
                t_parts = [pieces[n - 1]]
                if n >= NP - 1:
                    t_parts = halves(pieces[n - 1])
                if n == NP:
                    t_parts = t_parts[:1] + halves(t_parts[1])
                for cols in t_parts:
                    candidate(0, cols)
                    renew(0, cols)
        scatter_and_store(0)

        for cols in pieces:
            (z1_bank,) = matmul_group(wzr_sb, [(P, cols)], x_block, range(KB))
            update_gate(1, z1_bank, cols)
        for cols in pieces:
            candidate(1, cols)
        def in_psum(source):
            width = source.shape[-1]
            bank = psum.tile([P, PIECE], F32, name="bank")[:, :width]
            nc.tensor.matmul(bank, identity[:], source, start=True, stop=True)
            return bank

        gpsimd_cols = -(-2 * N // (3 * P)) * P
        gpsimd_part = slice(0, gpsimd_cols)
        vector_parts = [slice(c, min(c + PIECE, N)) for c in range(gpsimd_cols, N, PIECE)]
        h1_banks = [in_psum(x_f32[:, 1, cols]) for cols in pieces]
        z1_banks = [in_psum(z[1][:, cols]) for cols in vector_parts]
        nc.gpsimd.tensor_tensor(fresh[1][:, gpsimd_part], z[1][:, gpsimd_part], t[1][:, gpsimd_part], mult)
        for h1_bank, cols in zip(h1_banks, pieces):
            nc.vector.tensor_tensor(kept[1][:, cols], one_minus_z[1][:, cols], h1_bank, mult)
        for z1_bank, cols in zip(z1_banks, vector_parts):
            nc.vector.tensor_tensor(fresh[1][:, cols], t[1][:, cols], z1_bank, mult)
        scatter_and_store(1)
